import numpy as np
import ml_dtypes


def mxq(x, axis, fmt="e4m3"):
    dtype, down = {"e4m3": (ml_dtypes.float8_e4m3fn, 7), "e5m2": (ml_dtypes.float8_e5m2, 14)}[fmt]
    v = np.moveaxis(np.asarray(x, np.float32).astype(ml_dtypes.bfloat16).astype(np.float64), axis, -1)
    blocks = v.reshape(v.shape[:-1] + (-1, 32))
    amax = np.abs(blocks).max(-1, keepdims=True)
    byte = np.maximum(np.where(amax > 0, np.frexp(amax)[1] - 1 + 127, 0) - down, 1)
    scale = np.exp2(byte - 127.0)
    codes = (blocks / scale).astype(np.float32).astype(dtype).astype(np.float64)
    return np.moveaxis((codes * scale).reshape(v.shape), -1, axis)


WIDE = False


def mx_kscale(k):
    if not WIDE:
        return np.ones(k)
    levels = np.array([10, -10, 5, -5, 0])
    a = np.random.permutation(np.resize(levels, k // 512 * 4)).reshape(k // 512, 4)
    idx = np.arange(k)
    return np.exp2(a[idx // 512, idx % 128 // 32])


BF16 = ml_dtypes.bfloat16


def bf(x):
    return np.asarray(x, np.float32).astype(BF16)


def f64(x):
    return np.asarray(x).astype(np.float64)


B, L, S, D, DA, H, MLP = 2, 3, 1024, 512, 1024, 16, 4096
EPS = 1e-5


def layer_norm(u, g, b):
    mu = u.mean(-1, keepdims=True)
    var = ((u - mu) ** 2).mean(-1, keepdims=True)
    return (u - mu) / np.sqrt(var + EPS) * g + b


def grn(st, stq, W, b, g, be):
    w = np.maximum((stq @ mxq(f64(W), 0, "e4m3")).reshape(B, L, S, D) + f64(b), 0.0)
    n = layer_norm(st, f64(g), f64(be))
    return (w + n).sum(1)


def setup_inputs():
    s = mx_kscale(D)
    r = np.random.standard_normal
    return {"layer_outputs": bf(r((B, L, S, D)) * s),
            "grn_q_W": bf(r((D, D)) / np.sqrt(D) / s[:, None]), "grn_q_b": bf(r(D) * 0.2), "grn_q_g": bf(1.0 + 0.1 * r(D)), "grn_q_be": bf(r(D) * 0.1),
            "grn_k_W": bf(r((D, D)) / np.sqrt(D) / s[:, None]), "grn_k_b": bf(r(D) * 0.2), "grn_k_g": bf(1.0 + 0.1 * r(D)), "grn_k_be": bf(r(D) * 0.1),
            "grn_v_W": bf(r((D, D)) / np.sqrt(D) / s[:, None]), "grn_v_b": bf(r(D) * 0.2), "grn_v_g": bf(1.0 + 0.1 * r(D)), "grn_v_be": bf(r(D) * 0.1)}


def reference(layer_outputs, grn_q_W, grn_q_b, grn_q_g, grn_q_be, grn_k_W, grn_k_b, grn_k_g, grn_k_be, grn_v_W, grn_v_b, grn_v_g, grn_v_be):
    st = f64(layer_outputs)
    stq = mxq(st.reshape(B * L * S, D), 1, "e4m3")
    q = grn(st, stq, grn_q_W, grn_q_b, grn_q_g, grn_q_be)
    k = grn(st, stq, grn_k_W, grn_k_b, grn_k_g, grn_k_be)
    v = grn(st, stq, grn_v_W, grn_v_b, grn_v_g, grn_v_be)
    return q, k, v

@@ -1,0 +1,244 @@
+from contextlib import ExitStack
+
+import concourse.mybir as mybir
+from concourse.masks import make_identity
+
+F32 = mybir.dt.float32
+BF16 = mybir.dt.bfloat16
+U32 = mybir.dt.uint32
+U8 = mybir.dt.uint8
+FP8X4 = mybir.dt.float8_e4m3fn_x4
+ALU = mybir.AluOpType
+ACT = mybir.ActivationFunctionType
+
+BATCH, LAYERS, SEQ, D = 2, 3, 1024, 512
+EPS = 1e-5
+P = 128
+PACK = 4
+TILES = 4
+HALVES = SEQ // (P * TILES)
+BLOCKS = D // P
+KINDS = 3
+
+FLOPS = 2 * BATCH * LAYERS * SEQ * D * KINDS * D
+
+
+def tile_dcadecoderblock_pa_t_kernel(
+    tc,
+    layer_outputs,
+    grn_q_W, grn_q_b, grn_q_g, grn_q_be,
+    grn_k_W, grn_k_b, grn_k_g, grn_k_be,
+    grn_v_W, grn_v_b, grn_v_g, grn_v_be,
+    out_0, out_1, out_2,
+):
+    nc = tc.nc
+    weights = [grn_q_W, grn_k_W, grn_v_W]
+    vectors = [grn_q_b, grn_q_g, grn_q_be, grn_k_b, grn_k_g, grn_k_be, grn_v_b, grn_v_g, grn_v_be]
+    outs = [out_0, out_1, out_2]
+    groups = [(b, h) for b in range(BATCH) for h in range(HALVES)]
+
+    with ExitStack() as stack:
+        keep = stack.enter_context(tc.tile_pool(name="keep", bufs=1))
+        stage = stack.enter_context(tc.tile_pool(name="stage", bufs=2))
+        small = stack.enter_context(tc.tile_pool(name="small", bufs=6))
+        psum = stack.enter_context(tc.psum_pool(name="psum", bufs=1))
+
+        def rows_of_group(dram, h):
+            return dram.rearrange("(p h i) f -> p h i f", h=HALVES, i=TILES)[:, h]
+
+        w_raw = []
+        x_sb = {}
+
+        def load_weight(t):
+            raw = keep.tile([P, PACK, D], BF16, name="w_raw%d" % t)
+            for u in range(2):
+                nc.sync.dma_start(
+                    out=raw[:, 2 * u : 2 * u + 2, :],
+                    in_=weights[t][256 * u : 256 * u + 256, :].rearrange("(p e) c -> p e c", e=2),
+                )
+            w_raw.append(raw)
+
+        def load_group(g):
+            b, h = groups[g]
+            for l in range(LAYERS):
+                x = keep.tile([P, TILES, D], BF16, name="x%d_%d" % (g, l))
+                nc.sync.dma_start(out=x[:], in_=rows_of_group(layer_outputs[b, l], h))
+                x_sb[(g, l)] = x
+
+        load_weight(0)
+        load_group(0)
+        load_weight(1)
+        load_weight(2)
+        for g in range(1, len(groups)):
+            load_group(g)
+
+        ident_f = keep.tile([P, P], F32, name="ident_f")
+        make_identity(nc, ident_f[:])
+        ident_b = keep.tile([P, P], BF16, name="ident_b")
+        make_identity(nc, ident_b[:])
+        eps = keep.tile([P, 1], F32, name="eps")
+        nc.vector.memset(eps[:], EPS)
+
+        vec_rows = keep.tile([P, P], BF16, name="vec_rows")
+        nc.vector.memset(vec_rows[:], 0.0)
+        for n, vec in enumerate(vectors):
+            nc.scalar.dma_start(
+                out=vec_rows[BLOCKS * n : BLOCKS * n + BLOCKS, :],
+                in_=vec.rearrange("(j p) -> j p", p=P),
+            )
+        vec_ps = psum.tile([P, P], BF16, tag="xt", bufs=2, name="vec_ps")
+        nc.tensor.transpose(vec_ps[:], vec_rows[:], ident_b[:])
+        vec_cols = keep.tile([P, KINDS, 3, BLOCKS], F32, name="vec_cols")
+        nc.vector.tensor_copy(
+            out=vec_cols[:].rearrange("p t v j -> p (t v j)"), in_=vec_ps[:, 0 : KINDS * 3 * BLOCKS]
+        )
+        bias = vec_cols[:, :, 0, :]
+        gain = vec_cols[:, :, 1, :]
+        shift = vec_cols[:, :, 2, :]
+        neg_bias = keep.tile([P, KINDS, BLOCKS], F32, name="neg_bias")
+        nc.vector.tensor_scalar_mul(out=neg_bias[:], in0=bias, scalar1=-1.0)
+        rest = keep.tile([P, KINDS, BLOCKS], F32, name="rest")
+        nc.vector.tensor_scalar_mul(out=rest[:], in0=shift, scalar1=3.0)
+        nc.vector.scalar_tensor_tensor(
+            out=rest[:], in0=bias, scalar=2.0, in1=rest[:], op0=ALU.mult, op1=ALU.add
+        )
+
+        w_codes = []
+        w_scales = []
+        for t in range(KINDS):
+            grouped = stage.tile([P, D, PACK], BF16, align_bytes=64, name="w_grouped")
+            nc.vector.tensor_copy(
+                out=grouped[:].rearrange("p (c i) t -> p c t i", i=4),
+                in_=w_raw[t][:].rearrange("p t (c i) -> p c t i", i=4),
+            )
+            codes = keep.tile([P, D], U32, align_bytes=64, name="w_codes%d" % t)
+            scales = keep.tile([P, D], U8, align_bytes=64, name="w_scales%d" % t)
+            nc.vector.quantize_mx(
+                out=codes[:].bitcast(FP8X4),
+                scales=scales[:],
+                in_=grouped[:].rearrange("p c t -> p (c t)"),
+            )
+            w_codes.append(codes)
+            w_scales.append(scales)
+
+        for g in range(len(groups)):
+            b, h = groups[g]
+
+            x_codes = []
+            x_scales = []
+            for l in range(LAYERS):
+                words = x_sb[(g, l)][:].bitcast(F32)
+                grouped = stage.tile([P, TILES * P, PACK], BF16, align_bytes=64, bufs=3, name="x_grouped")
+                grouped_words = grouped[:].bitcast(F32)
+                for pair in range(TILES // 2):
+                    xt = psum.tile([P, 2, 2, P], F32, tag="xt", bufs=2, name="xt")
+                    for i in range(2):
+                        for u in range(2):
+                            nc.tensor.transpose(
+                                xt[:, i, u, :], words[:, 2 * pair + i, P * u : P * u + P], ident_f[:]
+                            )
+                    nc.scalar.copy(
+                        out=grouped_words[:, 2 * P * pair : 2 * P * pair + 2 * P, :].rearrange(
+                            "p (i r) u -> p i r u", i=2
+                        ),
+                        in_=xt[:].rearrange("p i u r -> p i r u"),
+                    )
+                codes = stage.tile([P, TILES * P], U32, align_bytes=64, bufs=6, name="x_codes")
+                scales = stage.tile([P, TILES * P], U8, align_bytes=64, bufs=6, name="x_scales")
+                nc.vector.quantize_mx(
+                    out=codes[:].bitcast(FP8X4),
+                    scales=scales[:],
+                    in_=grouped[:].rearrange("p n t -> p (n t)"),
+                )
+                x_codes.append(codes)
+                x_scales.append(scales)
+
+            normed = {}
+            for l in range(LAYERS):
+                stats = small.tile([P, TILES, 6], F32, name="stats")
+                mean_var = small.tile([P, TILES, 2], F32, name="mean_var")
+                for i in range(TILES):
+                    nc.vector.bn_stats(out=stats[:, i, :], in_=x_sb[(g, l)][:, i, :])
+                    nc.vector.bn_aggr(out=mean_var[:, i, :], in_=stats[:, i, :])
+                std = small.tile([P, TILES], F32, name="std")
+                nc.scalar.activation(out=std[:], in_=mean_var[:, :, 1], func=ACT.Sqrt, bias=eps[:], scale=1.0)
+                rstd = small.tile([P, TILES], F32, name="rstd")
+                nc.vector.reciprocal(out=rstd[:], in_=std[:])
+                mean_rstd = small.tile([P, TILES], F32, name="mean_rstd")
+                nc.vector.tensor_mul(out=mean_rstd[:], in0=mean_var[:, :, 0], in1=rstd[:])
+                for i in range(TILES):
+                    y = stage.tile([P, D], F32, bufs=LAYERS * TILES, name="normed")
+                    nc.gpsimd.tensor_scalar(
+                        out=y[:],
+                        in0=x_sb[(g, l)][:, i, :],
+                        scalar1=rstd[:, i : i + 1],
+                        scalar2=mean_rstd[:, i : i + 1],
+                        op0=ALU.mult,
+                        op1=ALU.subtract,
+                    )
+                    normed[(l, i)] = y
+
+            second = {}
+            for j in range(BLOCKS):
+                nt = psum.tile([P, TILES * P], F32, tag="nt", bufs=1, name="nt")
+                for i in range(TILES):
+                    for l in range(LAYERS):
+                        nc.tensor.matmul(
+                            out=nt[:, P * i : P * i + P],
+                            lhsT=normed[(l, i)][:, P * j : P * j + P],
+                            rhs=ident_f[:],
+                            is_transpose=True,
+                            start=(l == 0),
+                            stop=(l == LAYERS - 1),
+                        )
+                for t in range(KINDS):
+                    a = stage.tile([P, TILES * P], F32, bufs=16, name="second")
+                    nc.scalar.activation(
+                        out=a[:], in_=nt[:], func=ACT.Identity,
+                        scale=gain[:, t, j : j + 1], bias=rest[:, t, j : j + 1],
+                    )
+                    second[(t, j)] = a
+
+            for t in range(KINDS):
+                first = []
+                for j in range(BLOCKS):
+                    cols = slice(P * j, P * j + P)
+                    prods = []
+                    for l in range(LAYERS):
+                        prod = psum.tile([P, TILES * P], F32, tag="prod", bufs=3, name="prod")
+                        nc.tensor.matmul_mx(
+                            out=prod[:],
+                            lhsT=w_codes[t][:, cols].bitcast(FP8X4),
+                            lhsT_scale=w_scales[t][:, cols],
+                            rhs=x_codes[l][:].bitcast(FP8X4),
+                            rhs_scale=x_scales[l][:],
+                            start=True,
+                            stop=True,
+                        )
+                        prods.append(prod)
+                    acc = stage.tile([P, TILES * P], F32, bufs=8, name="first")
+                    nc.scalar.activation(
+                        out=acc[:], in_=prods[0][:], func=ACT.Relu, bias=bias[:, t, j : j + 1], scale=1.0
+                    )
+                    for l in range(1, LAYERS):
+                        nc.vector.scalar_tensor_tensor(
+                            out=acc[:], in0=prods[l][:], scalar=neg_bias[:, t, j : j + 1], in1=acc[:],
+                            op0=ALU.max, op1=ALU.add,
+                        )
+                    first.append(acc)
+
+                for i in range(TILES):
+                    back = psum.tile([P, D], F32, tag="back", bufs=2, name="back")
+                    for j in range(BLOCKS):
+                        for part, last in ((first[j], False), (second[(t, j)], True)):
+                            nc.tensor.matmul(
+                                out=back[:, P * j : P * j + P],
+                                lhsT=part[:, P * i : P * i + P],
+                                rhs=ident_f[:],
+                                is_transpose=True,
+                                start=not last,
+                                stop=last,
+                            )
+                    result = stage.tile([P, D], F32, bufs=6, name="result")
+                    nc.scalar.copy(out=result[:], in_=back[:])
+                    nc.sync.dma_start(out=rows_of_group(outs[t][b], h)[:, i], in_=result[:])

@@ -107,7 +107,7 @@ def tile_dcadecoderblock_pa_t_kernel(
         w_scales = []
         for t in range(KINDS):
             grouped = stage.tile([P, D, PACK], BF16, align_bytes=64, name="w_grouped")
-            nc.vector.tensor_copy(
+            nc.scalar.copy(
                 out=grouped[:].rearrange("p (c i) t -> p c t i", i=4),
                 in_=w_raw[t][:].rearrange("p t (c i) -> p c t i", i=4),
             )
@@ -168,7 +168,7 @@ def tile_dcadecoderblock_pa_t_kernel(
                 nc.vector.tensor_mul(out=mean_rstd[:], in0=mean_var[:, :, 0], in1=rstd[:])
                 for i in range(TILES):
                     y = stage.tile([P, D], F32, bufs=LAYERS * TILES, name="normed")
-                    nc.gpsimd.tensor_scalar(
+                    nc.vector.tensor_scalar(
                         out=y[:],
                         in0=x_sb[(g, l)][:, i, :],
                         scalar1=rstd[:, i : i + 1],

@@ -17,8 +17,23 @@ P = 128
 PACK = 4
 TILES = 4
 HALVES = SEQ // (P * TILES)
+GROUPS = BATCH * HALVES
 BLOCKS = D // P
 KINDS = 3
+PER_GROUP = BLOCKS * LAYERS
+STEPS = GROUPS * PER_GROUP
+
+LEAD_SEED = 3
+LEAD_NT = 6
+LEAD_SCALE = 19
+LEAD_RSTD = 22
+LEAD_STD = 23
+LEAD_STATS = 24
+LEAD_QUANTISE = 11
+LEAD_XT = 12
+LEAD_WEIGHTS = 14
+LEAD_CONSTANTS = 8
+LAG_BACK = PER_GROUP
 
 FLOPS = 2 * BATCH * LAYERS * SEQ * D * KINDS * D
 
@@ -35,21 +50,28 @@ def tile_dcadecoderblock_pa_t_kernel(
     weights = [grn_q_W, grn_k_W, grn_v_W]
     vectors = [grn_q_b, grn_q_g, grn_q_be, grn_k_b, grn_k_g, grn_k_be, grn_v_b, grn_v_g, grn_v_be]
     outs = [out_0, out_1, out_2]
-    groups = [(b, h) for b in range(BATCH) for h in range(HALVES)]
 
     with ExitStack() as stack:
+        stack.enter_context(tc.manual_schedule())
         keep = stack.enter_context(tc.tile_pool(name="keep", bufs=1))
         stage = stack.enter_context(tc.tile_pool(name="stage", bufs=2))
-        small = stack.enter_context(tc.tile_pool(name="small", bufs=6))
+        small = stack.enter_context(tc.tile_pool(name="small", bufs=4))
         psum = stack.enter_context(tc.psum_pool(name="psum", bufs=1))
 
-        def rows_of_group(dram, h):
-            return dram.rearrange("(p h i) f -> p h i f", h=HALVES, i=TILES)[:, h]
+        def rows_of_group(dram, g):
+            return dram[g // HALVES].rearrange("(p h i) f -> p h i f", h=HALVES, i=TILES)[:, g % HALVES]
 
-        w_raw = []
         x_sb = {}
 
-        def load_weight(t):
+        def load_group(g):
+            for l in range(LAYERS):
+                x = keep.tile([P, TILES, D], BF16, name="x%d_%d" % (g, l))
+                nc.sync.dma_start(out=x[:], in_=rows_of_group(layer_outputs[:, l], g))
+                x_sb[(g, l)] = x
+
+        load_group(0)
+        w_raw = []
+        for t in range(KINDS):
             raw = keep.tile([P, PACK, D], BF16, name="w_raw%d" % t)
             for u in range(2):
                 nc.sync.dma_start(
@@ -57,19 +79,14 @@ def tile_dcadecoderblock_pa_t_kernel(
                     in_=weights[t][256 * u : 256 * u + 256, :].rearrange("(p e) c -> p e c", e=2),
                 )
             w_raw.append(raw)
-
-        def load_group(g):
-            b, h = groups[g]
-            for l in range(LAYERS):
-                x = keep.tile([P, TILES, D], BF16, name="x%d_%d" % (g, l))
-                nc.sync.dma_start(out=x[:], in_=rows_of_group(layer_outputs[b, l], h))
-                x_sb[(g, l)] = x
-
-        load_weight(0)
-        load_group(0)
-        load_weight(1)
-        load_weight(2)
-        for g in range(1, len(groups)):
+        vec_rows = keep.tile([P, P], BF16, name="vec_rows")
+        nc.vector.memset(vec_rows[:], 0.0)
+        for n, vec in enumerate(vectors):
+            nc.sync.dma_start(
+                out=vec_rows[BLOCKS * n : BLOCKS * n + BLOCKS, :],
+                in_=vec.rearrange("(j p) -> j p", p=P),
+            )
+        for g in range(1, GROUPS):
             load_group(g)
 
         ident_f = keep.tile([P, P], F32, name="ident_f")
@@ -79,166 +96,218 @@ def tile_dcadecoderblock_pa_t_kernel(
         eps = keep.tile([P, 1], F32, name="eps")
         nc.vector.memset(eps[:], EPS)
 
-        vec_rows = keep.tile([P, P], BF16, name="vec_rows")
-        nc.vector.memset(vec_rows[:], 0.0)
-        for n, vec in enumerate(vectors):
-            nc.scalar.dma_start(
-                out=vec_rows[BLOCKS * n : BLOCKS * n + BLOCKS, :],
-                in_=vec.rearrange("(j p) -> j p", p=P),
-            )
-        vec_ps = psum.tile([P, P], BF16, tag="xt", bufs=2, name="vec_ps")
-        nc.tensor.transpose(vec_ps[:], vec_rows[:], ident_b[:])
         vec_cols = keep.tile([P, KINDS, 3, BLOCKS], F32, name="vec_cols")
-        nc.vector.tensor_copy(
-            out=vec_cols[:].rearrange("p t v j -> p (t v j)"), in_=vec_ps[:, 0 : KINDS * 3 * BLOCKS]
-        )
         bias = vec_cols[:, :, 0, :]
         gain = vec_cols[:, :, 1, :]
         shift = vec_cols[:, :, 2, :]
         neg_bias = keep.tile([P, KINDS, BLOCKS], F32, name="neg_bias")
-        nc.vector.tensor_scalar_mul(out=neg_bias[:], in0=bias, scalar1=-1.0)
         rest = keep.tile([P, KINDS, BLOCKS], F32, name="rest")
-        nc.vector.tensor_scalar_mul(out=rest[:], in0=shift, scalar1=3.0)
-        nc.vector.scalar_tensor_tensor(
-            out=rest[:], in0=bias, scalar=2.0, in1=rest[:], op0=ALU.mult, op1=ALU.add
-        )
 
-        w_codes = []
-        w_scales = []
-        for t in range(KINDS):
+        def split(index):
+            g, within = divmod(index, PER_GROUP)
+            a, c = divmod(within, LAYERS)
+            return g, a, c
+
+        def constants(index):
+            if index != 0:
+                return
+            vec_ps = psum.tile([P, P], BF16, tag="xt", name="vec_ps")
+            nc.tensor.transpose(vec_ps[:], vec_rows[:], ident_b[:])
+            nc.vector.tensor_copy(
+                out=vec_cols[:].rearrange("p t v j -> p (t v j)"), in_=vec_ps[:, 0 : KINDS * 3 * BLOCKS]
+            )
+            nc.vector.tensor_scalar_mul(out=neg_bias[:], in0=bias, scalar1=-1.0)
+            nc.vector.tensor_add(out=rest[:], in0=bias, in1=shift)
+            nc.vector.tensor_scalar_mul(out=rest[:], in0=rest[:], scalar1=3.0)
+
+        w_grouped = {}
+        w_codes = {}
+        w_scales = {}
+
+        def regroup_weight(t):
+            if not 0 <= t < KINDS:
+                return
             grouped = stage.tile([P, D, PACK], BF16, align_bytes=64, name="w_grouped")
             nc.scalar.copy(
                 out=grouped[:].rearrange("p (c i) t -> p c t i", i=4),
                 in_=w_raw[t][:].rearrange("p t (c i) -> p c t i", i=4),
             )
-            codes = keep.tile([P, D], U32, align_bytes=64, name="w_codes%d" % t)
-            scales = keep.tile([P, D], U8, align_bytes=64, name="w_scales%d" % t)
+            w_grouped[t] = grouped
+
+        def quantise_weight(t):
+            if not 0 <= t < KINDS:
+                return
+            w_codes[t] = keep.tile([P, D], U32, align_bytes=64, name="w_codes%d" % t)
+            w_scales[t] = keep.tile([P, D], U8, align_bytes=64, name="w_scales%d" % t)
             nc.vector.quantize_mx(
-                out=codes[:].bitcast(FP8X4),
-                scales=scales[:],
-                in_=grouped[:].rearrange("p c t -> p (c t)"),
+                out=w_codes[t][:].bitcast(FP8X4),
+                scales=w_scales[t][:],
+                in_=w_grouped[t][:].rearrange("p c t -> p (c t)"),
             )
-            w_codes.append(codes)
-            w_scales.append(scales)
 
-        for g in range(len(groups)):
-            b, h = groups[g]
+        x_grouped = {}
+        x_codes = {}
+        x_scales = {}
 
-            x_codes = []
-            x_scales = []
-            for l in range(LAYERS):
-                words = x_sb[(g, l)][:].bitcast(F32)
-                grouped = stage.tile([P, TILES * P, PACK], BF16, align_bytes=64, bufs=3, name="x_grouped")
-                grouped_words = grouped[:].bitcast(F32)
-                for pair in range(TILES // 2):
-                    xt = psum.tile([P, 2, 2, P], F32, tag="xt", bufs=2, name="xt")
-                    for i in range(2):
-                        for u in range(2):
-                            nc.tensor.transpose(
-                                xt[:, i, u, :], words[:, 2 * pair + i, P * u : P * u + P], ident_f[:]
-                            )
-                    nc.scalar.copy(
-                        out=grouped_words[:, 2 * P * pair : 2 * P * pair + 2 * P, :].rearrange(
-                            "p (i r) u -> p i r u", i=2
-                        ),
-                        in_=xt[:].rearrange("p i u r -> p i r u"),
-                    )
-                codes = stage.tile([P, TILES * P], U32, align_bytes=64, bufs=6, name="x_codes")
-                scales = stage.tile([P, TILES * P], U8, align_bytes=64, bufs=6, name="x_scales")
-                nc.vector.quantize_mx(
-                    out=codes[:].bitcast(FP8X4),
-                    scales=scales[:],
-                    in_=grouped[:].rearrange("p n t -> p (n t)"),
+        def transpose_x(index):
+            if not 0 <= index < STEPS:
+                return
+            g, i, l = split(index)
+            words = x_sb[(g, l)][:].bitcast(F32)
+            xt = psum.tile([P, 2, P], F32, tag="xt", name="xt")
+            for u in range(2):
+                nc.tensor.transpose(xt[:, u, :], words[:, i, P * u : P * u + P], ident_f[:])
+            grouped = stage.tile([P, P, PACK], BF16, align_bytes=64, bufs=3, name="x_grouped")
+            nc.scalar.copy(out=grouped[:].bitcast(F32), in_=xt[:].rearrange("p u r -> p r u"))
+            x_grouped[index] = grouped
+
+        def quantise_x(index):
+            if not 0 <= index < STEPS:
+                return
+            g, i, l = split(index)
+            if i == 0:
+                x_codes[(g, l)] = stage.tile([P, TILES * P], U32, align_bytes=64, bufs=6, name="x_codes")
+                x_scales[(g, l)] = stage.tile([P, TILES * P], U8, align_bytes=64, bufs=6, name="x_scales")
+            nc.vector.quantize_mx(
+                out=x_codes[(g, l)][:, P * i : P * i + P].bitcast(FP8X4),
+                scales=x_scales[(g, l)][:, P * i : P * i + P],
+                in_=x_grouped[index][:].rearrange("p r t -> p (r t)"),
+            )
+
+        stats = {}
+        mean_var = {}
+        std = {}
+        rstd = {}
+        offset = {}
+        normed = {}
+
+        def statistics(index):
+            if not 0 <= index < STEPS:
+                return
+            g, i, l = split(index)
+            if l == 0:
+                stats[(g, i)] = small.tile([P, LAYERS, 6], F32, name="stats")
+            nc.vector.bn_stats(out=stats[(g, i)][:, l, :], in_=x_sb[(g, l)][:, i, :])
+
+        def aggregate(index):
+            if not 0 <= index < STEPS:
+                return
+            g, i, l = split(index)
+            if l == 0:
+                mean_var[(g, i)] = small.tile([P, LAYERS, 2], F32, name="mean_var")
+            nc.vector.bn_aggr(out=mean_var[(g, i)][:, l, :], in_=stats[(g, i)][:, l, :])
+
+        def deviation(index):
+            if not 0 <= index < STEPS:
+                return
+            g, i, l = split(index)
+            if l == LAYERS - 1:
+                std[(g, i)] = small.tile([P, LAYERS], F32, name="std")
+                nc.scalar.activation(
+                    out=std[(g, i)][:], in_=mean_var[(g, i)][:, :, 1], func=ACT.Sqrt, bias=eps[:], scale=1.0
                 )
-                x_codes.append(codes)
-                x_scales.append(scales)
 
-            normed = {}
-            for l in range(LAYERS):
-                stats = small.tile([P, TILES, 6], F32, name="stats")
-                mean_var = small.tile([P, TILES, 2], F32, name="mean_var")
-                for i in range(TILES):
-                    nc.vector.bn_stats(out=stats[:, i, :], in_=x_sb[(g, l)][:, i, :])
-                    nc.vector.bn_aggr(out=mean_var[:, i, :], in_=stats[:, i, :])
-                std = small.tile([P, TILES], F32, name="std")
-                nc.scalar.activation(out=std[:], in_=mean_var[:, :, 1], func=ACT.Sqrt, bias=eps[:], scale=1.0)
-                rstd = small.tile([P, TILES], F32, name="rstd")
-                nc.vector.reciprocal(out=rstd[:], in_=std[:])
-                mean_rstd = small.tile([P, TILES], F32, name="mean_rstd")
-                nc.vector.tensor_mul(out=mean_rstd[:], in0=mean_var[:, :, 0], in1=rstd[:])
-                for i in range(TILES):
-                    y = stage.tile([P, D], F32, bufs=LAYERS * TILES, name="normed")
-                    nc.vector.tensor_scalar(
-                        out=y[:],
-                        in0=x_sb[(g, l)][:, i, :],
-                        scalar1=rstd[:, i : i + 1],
-                        scalar2=mean_rstd[:, i : i + 1],
-                        op0=ALU.mult,
-                        op1=ALU.subtract,
-                    )
-                    normed[(l, i)] = y
+        def reciprocal(index):
+            if not 0 <= index < STEPS:
+                return
+            g, i, l = split(index)
+            if l == LAYERS - 1:
+                rstd[(g, i)] = small.tile([P, LAYERS], F32, name="rstd")
+                nc.vector.reciprocal(out=rstd[(g, i)][:], in_=std[(g, i)][:])
+                offset[(g, i)] = small.tile([P, LAYERS], F32, name="offset")
+                nc.vector.scalar_tensor_tensor(
+                    out=offset[(g, i)][:], in0=mean_var[(g, i)][:, :, 0], scalar=-1.0, in1=rstd[(g, i)][:],
+                    op0=ALU.mult, op1=ALU.mult,
+                )
 
-            second = {}
-            for j in range(BLOCKS):
-                nt = psum.tile([P, TILES * P], F32, tag="nt", bufs=1, name="nt")
-                for i in range(TILES):
-                    for l in range(LAYERS):
-                        nc.tensor.matmul(
-                            out=nt[:, P * i : P * i + P],
-                            lhsT=normed[(l, i)][:, P * j : P * j + P],
-                            rhs=ident_f[:],
-                            is_transpose=True,
-                            start=(l == 0),
-                            stop=(l == LAYERS - 1),
-                        )
-                for t in range(KINDS):
-                    a = stage.tile([P, TILES * P], F32, bufs=16, name="second")
-                    nc.scalar.activation(
-                        out=a[:], in_=nt[:], func=ACT.Identity,
-                        scale=gain[:, t, j : j + 1], bias=rest[:, t, j : j + 1],
-                    )
-                    second[(t, j)] = a
+        def scale(index):
+            if not 0 <= index < STEPS:
+                return
+            g, i, l = split(index)
+            y = stage.tile([P, D], F32, bufs=2 * PER_GROUP, name="normed")
+            nc.gpsimd.tensor_scalar(
+                out=y[:], in0=x_sb[(g, l)][:, i, :],
+                scalar1=rstd[(g, i)][:, l : l + 1], scalar2=offset[(g, i)][:, l : l + 1],
+                op0=ALU.mult, op1=ALU.add,
+            )
+            normed[(g, i, l)] = y
 
+        nt = {}
+        acc = {}
+
+        def transpose_normed(index):
+            if not 0 <= index < STEPS:
+                return
+            g, j, third = split(index)
+            if third == 0:
+                nt[(g, j)] = psum.tile([P, TILES * P], F32, tag="nt", bufs=2, name="nt")
+            for n in range(TILES * third, TILES * third + TILES):
+                i, l = divmod(n, LAYERS)
+                nc.tensor.matmul(
+                    out=nt[(g, j)][:, P * i : P * i + P],
+                    lhsT=normed[(g, i, l)][:, P * j : P * j + P],
+                    rhs=ident_f[:],
+                    is_transpose=True,
+                    start=(l == 0),
+                    stop=(l == LAYERS - 1),
+                )
+
+        def seed(index):
+            if not 0 <= index < STEPS:
+                return
+            g, j, t = split(index)
+            a = stage.tile([P, TILES * P], F32, bufs=20, name="acc")
+            nc.scalar.activation(
+                out=a[:], in_=nt[(g, j)][:], func=ACT.Identity,
+                scale=gain[:, t, j : j + 1], bias=rest[:, t, j : j + 1],
+            )
+            acc[(g, t, j)] = a
+
+        def products(index):
+            if not 0 <= index < STEPS:
+                return
+            g, j, l = split(index)
+            cols = slice(P * j, P * j + P)
             for t in range(KINDS):
-                first = []
-                for j in range(BLOCKS):
-                    cols = slice(P * j, P * j + P)
-                    prods = []
-                    for l in range(LAYERS):
-                        prod = psum.tile([P, TILES * P], F32, tag="prod", bufs=3, name="prod")
-                        nc.tensor.matmul_mx(
-                            out=prod[:],
-                            lhsT=w_codes[t][:, cols].bitcast(FP8X4),
-                            lhsT_scale=w_scales[t][:, cols],
-                            rhs=x_codes[l][:].bitcast(FP8X4),
-                            rhs_scale=x_scales[l][:],
-                            start=True,
-                            stop=True,
-                        )
-                        prods.append(prod)
-                    acc = stage.tile([P, TILES * P], F32, bufs=8, name="first")
-                    nc.scalar.activation(
-                        out=acc[:], in_=prods[0][:], func=ACT.Relu, bias=bias[:, t, j : j + 1], scale=1.0
-                    )
-                    for l in range(1, LAYERS):
-                        nc.vector.scalar_tensor_tensor(
-                            out=acc[:], in0=prods[l][:], scalar=neg_bias[:, t, j : j + 1], in1=acc[:],
-                            op0=ALU.max, op1=ALU.add,
-                        )
-                    first.append(acc)
+                prod = psum.tile([P, TILES * P], F32, tag="prod", bufs=3, name="prod")
+                nc.tensor.matmul_mx(
+                    out=prod[:],
+                    lhsT=w_codes[t][:, cols].bitcast(FP8X4),
+                    lhsT_scale=w_scales[t][:, cols],
+                    rhs=x_codes[(g, l)][:].bitcast(FP8X4),
+                    rhs_scale=x_scales[(g, l)][:],
+                    start=True,
+                    stop=True,
+                )
+                nc.vector.scalar_tensor_tensor(
+                    out=acc[(g, t, j)][:], in0=prod[:], scalar=neg_bias[:, t, j : j + 1],
+                    in1=acc[(g, t, j)][:], op0=ALU.max, op1=ALU.add,
+                )
 
-                for i in range(TILES):
-                    back = psum.tile([P, D], F32, tag="back", bufs=2, name="back")
-                    for j in range(BLOCKS):
-                        for part, last in ((first[j], False), (second[(t, j)], True)):
-                            nc.tensor.matmul(
-                                out=back[:, P * j : P * j + P],
-                                lhsT=part[:, P * i : P * i + P],
-                                rhs=ident_f[:],
-                                is_transpose=True,
-                                start=not last,
-                                stop=last,
-                            )
-                    result = stage.tile([P, D], F32, bufs=6, name="result")
-                    nc.scalar.copy(out=result[:], in_=back[:])
-                    nc.sync.dma_start(out=rows_of_group(outs[t][b], h)[:, i], in_=result[:])
+        def back(index):
+            if not 0 <= index < STEPS:
+                return
+            g, within = divmod(index, PER_GROUP)
+            t, i = divmod(within, TILES)
+            turned = psum.tile([P, D], F32, tag="back", bufs=2, name="turned")
+            for j in range(BLOCKS):
+                nc.tensor.transpose(turned[:, P * j : P * j + P], acc[(g, t, j)][:, P * i : P * i + P], ident_f[:])
+            result = stage.tile([P, D], F32, bufs=4, name="result")
+            nc.scalar.copy(out=result[:], in_=turned[:])
+            nc.sync.dma_start(out=rows_of_group(outs[t], g)[:, i], in_=result[:])
+
+        for step in range(-LEAD_STATS, STEPS + LAG_BACK):
+            products(step)
+            deviation(step + LEAD_STD)
+            seed(step + LEAD_SEED)
+            back(step - LAG_BACK)
+            transpose_normed(step + LEAD_NT)
+            transpose_x(step + LEAD_XT)
+            regroup_weight(step + LEAD_WEIGHTS)
+            constants(step + LEAD_CONSTANTS)
+            statistics(step + LEAD_STATS)
+            quantise_x(step + LEAD_QUANTISE)
+            quantise_weight(step + LEAD_WEIGHTS - 1)
+            aggregate(step + LEAD_STATS)
+            reciprocal(step + LEAD_RSTD)
+            scale(step + LEAD_SCALE)

@@ -17,23 +17,8 @@ P = 128
 PACK = 4
 TILES = 4
 HALVES = SEQ // (P * TILES)
-GROUPS = BATCH * HALVES
 BLOCKS = D // P
 KINDS = 3
-PER_GROUP = BLOCKS * LAYERS
-STEPS = GROUPS * PER_GROUP
-
-LEAD_SEED = 3
-LEAD_NT = 6
-LEAD_SCALE = 19
-LEAD_RSTD = 22
-LEAD_STD = 23
-LEAD_STATS = 24
-LEAD_QUANTISE = 11
-LEAD_XT = 12
-LEAD_WEIGHTS = 14
-LEAD_CONSTANTS = 8
-LAG_BACK = PER_GROUP
 
 FLOPS = 2 * BATCH * LAYERS * SEQ * D * KINDS * D
 
@@ -50,28 +35,21 @@ def tile_dcadecoderblock_pa_t_kernel(
     weights = [grn_q_W, grn_k_W, grn_v_W]
     vectors = [grn_q_b, grn_q_g, grn_q_be, grn_k_b, grn_k_g, grn_k_be, grn_v_b, grn_v_g, grn_v_be]
     outs = [out_0, out_1, out_2]
+    groups = [(b, h) for b in range(BATCH) for h in range(HALVES)]
 
     with ExitStack() as stack:
-        stack.enter_context(tc.manual_schedule())
         keep = stack.enter_context(tc.tile_pool(name="keep", bufs=1))
         stage = stack.enter_context(tc.tile_pool(name="stage", bufs=2))
-        small = stack.enter_context(tc.tile_pool(name="small", bufs=4))
+        small = stack.enter_context(tc.tile_pool(name="small", bufs=6))
         psum = stack.enter_context(tc.psum_pool(name="psum", bufs=1))
 
-        def rows_of_group(dram, g):
-            return dram[g // HALVES].rearrange("(p h i) f -> p h i f", h=HALVES, i=TILES)[:, g % HALVES]
+        def rows_of_group(dram, h):
+            return dram.rearrange("(p h i) f -> p h i f", h=HALVES, i=TILES)[:, h]
 
+        w_raw = []
         x_sb = {}
 
-        def load_group(g):
-            for l in range(LAYERS):
-                x = keep.tile([P, TILES, D], BF16, name="x%d_%d" % (g, l))
-                nc.sync.dma_start(out=x[:], in_=rows_of_group(layer_outputs[:, l], g))
-                x_sb[(g, l)] = x
-
-        load_group(0)
-        w_raw = []
-        for t in range(KINDS):
+        def load_weight(t):
             raw = keep.tile([P, PACK, D], BF16, name="w_raw%d" % t)
             for u in range(2):
                 nc.sync.dma_start(
@@ -79,14 +57,27 @@ def tile_dcadecoderblock_pa_t_kernel(
                     in_=weights[t][256 * u : 256 * u + 256, :].rearrange("(p e) c -> p e c", e=2),
                 )
             w_raw.append(raw)
+
+        def load_group(g):
+            b, h = groups[g]
+            for l in range(LAYERS):
+                x = keep.tile([P, TILES, D], BF16, name="x%d_%d" % (g, l))
+                nc.sync.dma_start(out=x[:], in_=rows_of_group(layer_outputs[b, l], h))
+                x_sb[(g, l)] = x
+
         vec_rows = keep.tile([P, P], BF16, name="vec_rows")
         nc.vector.memset(vec_rows[:], 0.0)
+
+        load_weight(0)
+        load_group(0)
         for n, vec in enumerate(vectors):
             nc.sync.dma_start(
                 out=vec_rows[BLOCKS * n : BLOCKS * n + BLOCKS, :],
                 in_=vec.rearrange("(j p) -> j p", p=P),
             )
-        for g in range(1, GROUPS):
+        load_weight(1)
+        load_weight(2)
+        for g in range(1, len(groups)):
             load_group(g)
 
         ident_f = keep.tile([P, P], F32, name="ident_f")
@@ -96,218 +87,156 @@ def tile_dcadecoderblock_pa_t_kernel(
         eps = keep.tile([P, 1], F32, name="eps")
         nc.vector.memset(eps[:], EPS)
 
+        vec_ps = psum.tile([P, P], BF16, tag="xt", bufs=1, name="vec_ps")
+        nc.tensor.transpose(vec_ps[:], vec_rows[:], ident_b[:])
         vec_cols = keep.tile([P, KINDS, 3, BLOCKS], F32, name="vec_cols")
+        nc.vector.tensor_copy(
+            out=vec_cols[:].rearrange("p t v j -> p (t v j)"), in_=vec_ps[:, 0 : KINDS * 3 * BLOCKS]
+        )
         bias = vec_cols[:, :, 0, :]
         gain = vec_cols[:, :, 1, :]
         shift = vec_cols[:, :, 2, :]
         neg_bias = keep.tile([P, KINDS, BLOCKS], F32, name="neg_bias")
+        nc.vector.tensor_scalar_mul(out=neg_bias[:], in0=bias, scalar1=-1.0)
         rest = keep.tile([P, KINDS, BLOCKS], F32, name="rest")
+        nc.vector.tensor_add(out=rest[:], in0=bias, in1=shift)
+        nc.vector.tensor_scalar_mul(out=rest[:], in0=rest[:], scalar1=3.0)
 
-        def split(index):
-            g, within = divmod(index, PER_GROUP)
-            a, c = divmod(within, LAYERS)
-            return g, a, c
-
-        def constants(index):
-            if index != 0:
-                return
-            vec_ps = psum.tile([P, P], BF16, tag="xt", name="vec_ps")
-            nc.tensor.transpose(vec_ps[:], vec_rows[:], ident_b[:])
-            nc.vector.tensor_copy(
-                out=vec_cols[:].rearrange("p t v j -> p (t v j)"), in_=vec_ps[:, 0 : KINDS * 3 * BLOCKS]
-            )
-            nc.vector.tensor_scalar_mul(out=neg_bias[:], in0=bias, scalar1=-1.0)
-            nc.vector.tensor_add(out=rest[:], in0=bias, in1=shift)
-            nc.vector.tensor_scalar_mul(out=rest[:], in0=rest[:], scalar1=3.0)
-
-        w_grouped = {}
-        w_codes = {}
-        w_scales = {}
-
-        def regroup_weight(t):
-            if not 0 <= t < KINDS:
-                return
+        w_codes = []
+        w_scales = []
+        for t in range(KINDS):
             grouped = stage.tile([P, D, PACK], BF16, align_bytes=64, name="w_grouped")
             nc.scalar.copy(
                 out=grouped[:].rearrange("p (c i) t -> p c t i", i=4),
                 in_=w_raw[t][:].rearrange("p t (c i) -> p c t i", i=4),
             )
-            w_grouped[t] = grouped
-
-        def quantise_weight(t):
-            if not 0 <= t < KINDS:
-                return
-            w_codes[t] = keep.tile([P, D], U32, align_bytes=64, name="w_codes%d" % t)
-            w_scales[t] = keep.tile([P, D], U8, align_bytes=64, name="w_scales%d" % t)
+            codes = keep.tile([P, D], U32, align_bytes=64, name="w_codes%d" % t)
+            scales = keep.tile([P, D], U8, align_bytes=64, name="w_scales%d" % t)
             nc.vector.quantize_mx(
-                out=w_codes[t][:].bitcast(FP8X4),
-                scales=w_scales[t][:],
-                in_=w_grouped[t][:].rearrange("p c t -> p (c t)"),
+                out=codes[:].bitcast(FP8X4),
+                scales=scales[:],
+                in_=grouped[:].rearrange("p c t -> p (c t)"),
             )
+            w_codes.append(codes)
+            w_scales.append(scales)
 
-        x_grouped = {}
         x_codes = {}
         x_scales = {}
-
-        def transpose_x(index):
-            if not 0 <= index < STEPS:
-                return
-            g, i, l = split(index)
-            words = x_sb[(g, l)][:].bitcast(F32)
-            xt = psum.tile([P, 2, P], F32, tag="xt", name="xt")
-            for u in range(2):
-                nc.tensor.transpose(xt[:, u, :], words[:, i, P * u : P * u + P], ident_f[:])
-            grouped = stage.tile([P, P, PACK], BF16, align_bytes=64, bufs=3, name="x_grouped")
-            nc.scalar.copy(out=grouped[:].bitcast(F32), in_=xt[:].rearrange("p u r -> p r u"))
-            x_grouped[index] = grouped
-
-        def quantise_x(index):
-            if not 0 <= index < STEPS:
-                return
-            g, i, l = split(index)
-            if i == 0:
-                x_codes[(g, l)] = stage.tile([P, TILES * P], U32, align_bytes=64, bufs=6, name="x_codes")
-                x_scales[(g, l)] = stage.tile([P, TILES * P], U8, align_bytes=64, bufs=6, name="x_scales")
-            nc.vector.quantize_mx(
-                out=x_codes[(g, l)][:, P * i : P * i + P].bitcast(FP8X4),
-                scales=x_scales[(g, l)][:, P * i : P * i + P],
-                in_=x_grouped[index][:].rearrange("p r t -> p (r t)"),
-            )
-
-        stats = {}
-        mean_var = {}
-        std = {}
-        rstd = {}
-        offset = {}
         normed = {}
-
-        def statistics(index):
-            if not 0 <= index < STEPS:
-                return
-            g, i, l = split(index)
-            if l == 0:
-                stats[(g, i)] = small.tile([P, LAYERS, 6], F32, name="stats")
-            nc.vector.bn_stats(out=stats[(g, i)][:, l, :], in_=x_sb[(g, l)][:, i, :])
-
-        def aggregate(index):
-            if not 0 <= index < STEPS:
-                return
-            g, i, l = split(index)
-            if l == 0:
-                mean_var[(g, i)] = small.tile([P, LAYERS, 2], F32, name="mean_var")
-            nc.vector.bn_aggr(out=mean_var[(g, i)][:, l, :], in_=stats[(g, i)][:, l, :])
-
-        def deviation(index):
-            if not 0 <= index < STEPS:
-                return
-            g, i, l = split(index)
-            if l == LAYERS - 1:
-                std[(g, i)] = small.tile([P, LAYERS], F32, name="std")
-                nc.scalar.activation(
-                    out=std[(g, i)][:], in_=mean_var[(g, i)][:, :, 1], func=ACT.Sqrt, bias=eps[:], scale=1.0
-                )
-
-        def reciprocal(index):
-            if not 0 <= index < STEPS:
-                return
-            g, i, l = split(index)
-            if l == LAYERS - 1:
-                rstd[(g, i)] = small.tile([P, LAYERS], F32, name="rstd")
-                nc.vector.reciprocal(out=rstd[(g, i)][:], in_=std[(g, i)][:])
-                offset[(g, i)] = small.tile([P, LAYERS], F32, name="offset")
-                nc.vector.scalar_tensor_tensor(
-                    out=offset[(g, i)][:], in0=mean_var[(g, i)][:, :, 0], scalar=-1.0, in1=rstd[(g, i)][:],
-                    op0=ALU.mult, op1=ALU.mult,
-                )
-
-        def scale(index):
-            if not 0 <= index < STEPS:
-                return
-            g, i, l = split(index)
-            y = stage.tile([P, D], F32, bufs=2 * PER_GROUP, name="normed")
-            nc.gpsimd.tensor_scalar(
-                out=y[:], in0=x_sb[(g, l)][:, i, :],
-                scalar1=rstd[(g, i)][:, l : l + 1], scalar2=offset[(g, i)][:, l : l + 1],
-                op0=ALU.mult, op1=ALU.add,
-            )
-            normed[(g, i, l)] = y
-
-        nt = {}
         acc = {}
 
-        def transpose_normed(index):
-            if not 0 <= index < STEPS:
-                return
-            g, j, third = split(index)
-            if third == 0:
-                nt[(g, j)] = psum.tile([P, TILES * P], F32, tag="nt", bufs=2, name="nt")
-            for n in range(TILES * third, TILES * third + TILES):
-                i, l = divmod(n, LAYERS)
-                nc.tensor.matmul(
-                    out=nt[(g, j)][:, P * i : P * i + P],
-                    lhsT=normed[(g, i, l)][:, P * j : P * j + P],
-                    rhs=ident_f[:],
-                    is_transpose=True,
-                    start=(l == 0),
-                    stop=(l == LAYERS - 1),
+        def quantise_group(g):
+            for l in range(LAYERS):
+                words = x_sb[(g, l)][:].bitcast(F32)
+                grouped = stage.tile([P, TILES * P, PACK], BF16, align_bytes=64, bufs=3, name="x_grouped")
+                grouped_words = grouped[:].bitcast(F32)
+                for pair in range(TILES // 2):
+                    xt = psum.tile([P, 2, 2, P], F32, tag="xt", bufs=1, name="xt")
+                    for i in range(2):
+                        for u in range(2):
+                            nc.tensor.transpose(
+                                xt[:, i, u, :], words[:, 2 * pair + i, P * u : P * u + P], ident_f[:]
+                            )
+                    nc.scalar.copy(
+                        out=grouped_words[:, 2 * P * pair : 2 * P * pair + 2 * P, :].rearrange(
+                            "p (i r) u -> p i r u", i=2
+                        ),
+                        in_=xt[:].rearrange("p i u r -> p i r u"),
+                    )
+                codes = stage.tile([P, TILES * P], U32, align_bytes=64, bufs=6, name="x_codes")
+                scales = stage.tile([P, TILES * P], U8, align_bytes=64, bufs=6, name="x_scales")
+                nc.vector.quantize_mx(
+                    out=codes[:].bitcast(FP8X4),
+                    scales=scales[:],
+                    in_=grouped[:].rearrange("p n t -> p (n t)"),
                 )
+                x_codes[(g, l)] = codes
+                x_scales[(g, l)] = scales
 
-        def seed(index):
-            if not 0 <= index < STEPS:
-                return
-            g, j, t = split(index)
-            a = stage.tile([P, TILES * P], F32, bufs=20, name="acc")
-            nc.scalar.activation(
-                out=a[:], in_=nt[(g, j)][:], func=ACT.Identity,
-                scale=gain[:, t, j : j + 1], bias=rest[:, t, j : j + 1],
-            )
-            acc[(g, t, j)] = a
-
-        def products(index):
-            if not 0 <= index < STEPS:
-                return
-            g, j, l = split(index)
-            cols = slice(P * j, P * j + P)
-            for t in range(KINDS):
-                prod = psum.tile([P, TILES * P], F32, tag="prod", bufs=3, name="prod")
-                nc.tensor.matmul_mx(
-                    out=prod[:],
-                    lhsT=w_codes[t][:, cols].bitcast(FP8X4),
-                    lhsT_scale=w_scales[t][:, cols],
-                    rhs=x_codes[(g, l)][:].bitcast(FP8X4),
-                    rhs_scale=x_scales[(g, l)][:],
-                    start=True,
-                    stop=True,
-                )
+        def normalise_group(g):
+            for l in range(LAYERS):
+                stats = small.tile([P, TILES, 6], F32, name="stats")
+                mean_var = small.tile([P, TILES, 2], F32, name="mean_var")
+                for i in range(TILES):
+                    nc.vector.bn_stats(out=stats[:, i, :], in_=x_sb[(g, l)][:, i, :])
+                for i in range(TILES):
+                    nc.vector.bn_aggr(out=mean_var[:, i, :], in_=stats[:, i, :])
+                std = small.tile([P, TILES], F32, name="std")
+                nc.scalar.activation(out=std[:], in_=mean_var[:, :, 1], func=ACT.Sqrt, bias=eps[:], scale=1.0)
+                rstd = small.tile([P, TILES], F32, name="rstd")
+                nc.vector.reciprocal(out=rstd[:], in_=std[:])
+                offset = small.tile([P, TILES], F32, name="offset")
                 nc.vector.scalar_tensor_tensor(
-                    out=acc[(g, t, j)][:], in0=prod[:], scalar=neg_bias[:, t, j : j + 1],
-                    in1=acc[(g, t, j)][:], op0=ALU.max, op1=ALU.add,
+                    out=offset[:], in0=mean_var[:, :, 0], scalar=-1.0, in1=rstd[:], op0=ALU.mult, op1=ALU.mult
                 )
+                for i in range(TILES):
+                    y = stage.tile([P, D], F32, bufs=2 * LAYERS * TILES, name="normed")
+                    nc.gpsimd.tensor_scalar(
+                        out=y[:], in0=x_sb[(g, l)][:, i, :],
+                        scalar1=rstd[:, i : i + 1], scalar2=offset[:, i : i + 1],
+                        op0=ALU.mult, op1=ALU.add,
+                    )
+                    normed[(g, l, i)] = y
 
-        def back(index):
-            if not 0 <= index < STEPS:
-                return
-            g, within = divmod(index, PER_GROUP)
-            t, i = divmod(within, TILES)
-            turned = psum.tile([P, D], F32, tag="back", bufs=2, name="turned")
+        def seed_group(g):
             for j in range(BLOCKS):
-                nc.tensor.transpose(turned[:, P * j : P * j + P], acc[(g, t, j)][:, P * i : P * i + P], ident_f[:])
-            result = stage.tile([P, D], F32, bufs=4, name="result")
-            nc.scalar.copy(out=result[:], in_=turned[:])
-            nc.sync.dma_start(out=rows_of_group(outs[t], g)[:, i], in_=result[:])
+                nt = psum.tile([P, TILES * P], F32, tag="nt", bufs=2, name="nt")
+                for i in range(TILES):
+                    for l in range(LAYERS):
+                        nc.tensor.matmul(
+                            out=nt[:, P * i : P * i + P],
+                            lhsT=normed[(g, l, i)][:, P * j : P * j + P],
+                            rhs=ident_f[:],
+                            is_transpose=True,
+                            start=(l == 0),
+                            stop=(l == LAYERS - 1),
+                        )
+                for t in range(KINDS):
+                    a = stage.tile([P, TILES * P], F32, bufs=2 * KINDS * BLOCKS, name="acc")
+                    nc.scalar.activation(
+                        out=a[:], in_=nt[:], func=ACT.Identity,
+                        scale=gain[:, t, j : j + 1], bias=rest[:, t, j : j + 1],
+                    )
+                    acc[(g, t, j)] = a
 
-        for step in range(-LEAD_STATS, STEPS + LAG_BACK):
-            products(step)
-            deviation(step + LEAD_STD)
-            seed(step + LEAD_SEED)
-            back(step - LAG_BACK)
-            transpose_normed(step + LEAD_NT)
-            transpose_x(step + LEAD_XT)
-            regroup_weight(step + LEAD_WEIGHTS)
-            constants(step + LEAD_CONSTANTS)
-            statistics(step + LEAD_STATS)
-            quantise_x(step + LEAD_QUANTISE)
-            quantise_weight(step + LEAD_WEIGHTS - 1)
-            aggregate(step + LEAD_STATS)
-            reciprocal(step + LEAD_RSTD)
-            scale(step + LEAD_SCALE)
+        def products_group(g):
+            b, h = groups[g]
+            for t in range(KINDS):
+                for l in range(LAYERS):
+                    for j in range(BLOCKS):
+                        cols = slice(P * j, P * j + P)
+                        prod = psum.tile([P, TILES * P], F32, tag="prod", bufs=3, name="prod")
+                        nc.tensor.matmul_mx(
+                            out=prod[:],
+                            lhsT=w_codes[t][:, cols].bitcast(FP8X4),
+                            lhsT_scale=w_scales[t][:, cols],
+                            rhs=x_codes[(g, l)][:].bitcast(FP8X4),
+                            rhs_scale=x_scales[(g, l)][:],
+                            start=True,
+                            stop=True,
+                        )
+                        nc.vector.scalar_tensor_tensor(
+                            out=acc[(g, t, j)][:], in0=prod[:], scalar=neg_bias[:, t, j : j + 1],
+                            in1=acc[(g, t, j)][:], op0=ALU.max, op1=ALU.add,
+                        )
+                for i in range(TILES):
+                    back = psum.tile([P, D], F32, tag="back", bufs=2, name="back")
+                    for j in range(BLOCKS):
+                        nc.tensor.transpose(
+                            back[:, P * j : P * j + P], acc[(g, t, j)][:, P * i : P * i + P], ident_f[:]
+                        )
+                    result = stage.tile([P, D], F32, bufs=6, name="result")
+                    nc.scalar.copy(out=result[:], in_=back[:])
+                    nc.sync.dma_start(out=rows_of_group(outs[t][b], h)[:, i], in_=result[:])
+
+        normalise_group(0)
+        normalise_group(1)
+        quantise_group(0)
+        seed_group(0)
+        for g in range(len(groups)):
+            if g + 2 < len(groups):
+                normalise_group(g + 2)
+            if g + 1 < len(groups):
+                quantise_group(g + 1)
+                seed_group(g + 1)
+            products_group(g)

@@ -17,8 +17,23 @@ P = 128
 PACK = 4
 TILES = 4
 HALVES = SEQ // (P * TILES)
+GROUPS = BATCH * HALVES
 BLOCKS = D // P
 KINDS = 3
+PER_GROUP = BLOCKS * LAYERS
+STEPS = GROUPS * PER_GROUP
+
+LEAD_SEED = 3
+LEAD_NT = 6
+LEAD_SCALE = 19
+LEAD_RSTD = 22
+LEAD_STD = 23
+LEAD_STATS = 24
+LEAD_QUANTISE = 11
+LEAD_XT = 12
+LEAD_WEIGHTS = 14
+LEAD_CONSTANTS = 8
+LAG_BACK = 3
 
 FLOPS = 2 * BATCH * LAYERS * SEQ * D * KINDS * D
 
@@ -35,21 +50,28 @@ def tile_dcadecoderblock_pa_t_kernel(
     weights = [grn_q_W, grn_k_W, grn_v_W]
     vectors = [grn_q_b, grn_q_g, grn_q_be, grn_k_b, grn_k_g, grn_k_be, grn_v_b, grn_v_g, grn_v_be]
     outs = [out_0, out_1, out_2]
-    groups = [(b, h) for b in range(BATCH) for h in range(HALVES)]
 
     with ExitStack() as stack:
+        stack.enter_context(tc.manual_schedule())
         keep = stack.enter_context(tc.tile_pool(name="keep", bufs=1))
         stage = stack.enter_context(tc.tile_pool(name="stage", bufs=2))
-        small = stack.enter_context(tc.tile_pool(name="small", bufs=6))
+        small = stack.enter_context(tc.tile_pool(name="small", bufs=4))
         psum = stack.enter_context(tc.psum_pool(name="psum", bufs=1))
 
-        def rows_of_group(dram, h):
-            return dram.rearrange("(p h i) f -> p h i f", h=HALVES, i=TILES)[:, h]
+        def rows_of_group(dram, g):
+            return dram[g // HALVES].rearrange("(p h i) f -> p h i f", h=HALVES, i=TILES)[:, g % HALVES]
 
-        w_raw = []
         x_sb = {}
 
-        def load_weight(t):
+        def load_group(g):
+            for l in range(LAYERS):
+                x = keep.tile([P, TILES, D], BF16, name="x%d_%d" % (g, l))
+                nc.sync.dma_start(out=x[:], in_=rows_of_group(layer_outputs[:, l], g))
+                x_sb[(g, l)] = x
+
+        load_group(0)
+        w_raw = []
+        for t in range(KINDS):
             raw = keep.tile([P, PACK, D], BF16, name="w_raw%d" % t)
             for u in range(2):
                 nc.sync.dma_start(
@@ -57,27 +79,14 @@ def tile_dcadecoderblock_pa_t_kernel(
                     in_=weights[t][256 * u : 256 * u + 256, :].rearrange("(p e) c -> p e c", e=2),
                 )
             w_raw.append(raw)
-
-        def load_group(g):
-            b, h = groups[g]
-            for l in range(LAYERS):
-                x = keep.tile([P, TILES, D], BF16, name="x%d_%d" % (g, l))
-                nc.sync.dma_start(out=x[:], in_=rows_of_group(layer_outputs[b, l], h))
-                x_sb[(g, l)] = x
-
         vec_rows = keep.tile([P, P], BF16, name="vec_rows")
         nc.vector.memset(vec_rows[:], 0.0)
-
-        load_weight(0)
-        load_group(0)
         for n, vec in enumerate(vectors):
             nc.sync.dma_start(
                 out=vec_rows[BLOCKS * n : BLOCKS * n + BLOCKS, :],
                 in_=vec.rearrange("(j p) -> j p", p=P),
             )
-        load_weight(1)
-        load_weight(2)
-        for g in range(1, len(groups)):
+        for g in range(1, GROUPS):
             load_group(g)
 
         ident_f = keep.tile([P, P], F32, name="ident_f")
@@ -87,156 +96,217 @@ def tile_dcadecoderblock_pa_t_kernel(
         eps = keep.tile([P, 1], F32, name="eps")
         nc.vector.memset(eps[:], EPS)
 
-        vec_ps = psum.tile([P, P], BF16, tag="xt", bufs=1, name="vec_ps")
-        nc.tensor.transpose(vec_ps[:], vec_rows[:], ident_b[:])
         vec_cols = keep.tile([P, KINDS, 3, BLOCKS], F32, name="vec_cols")
-        nc.vector.tensor_copy(
-            out=vec_cols[:].rearrange("p t v j -> p (t v j)"), in_=vec_ps[:, 0 : KINDS * 3 * BLOCKS]
-        )
         bias = vec_cols[:, :, 0, :]
         gain = vec_cols[:, :, 1, :]
         shift = vec_cols[:, :, 2, :]
         neg_bias = keep.tile([P, KINDS, BLOCKS], F32, name="neg_bias")
-        nc.vector.tensor_scalar_mul(out=neg_bias[:], in0=bias, scalar1=-1.0)
         rest = keep.tile([P, KINDS, BLOCKS], F32, name="rest")
-        nc.vector.tensor_add(out=rest[:], in0=bias, in1=shift)
-        nc.vector.tensor_scalar_mul(out=rest[:], in0=rest[:], scalar1=3.0)
 
-        w_codes = []
-        w_scales = []
-        for t in range(KINDS):
+        def split(index):
+            g, within = divmod(index, PER_GROUP)
+            a, c = divmod(within, LAYERS)
+            return g, a, c
+
+        def constants(index):
+            if index != 0:
+                return
+            vec_ps = psum.tile([P, P], BF16, tag="xt", name="vec_ps")
+            nc.tensor.transpose(vec_ps[:], vec_rows[:], ident_b[:])
+            nc.vector.tensor_copy(
+                out=vec_cols[:].rearrange("p t v j -> p (t v j)"), in_=vec_ps[:, 0 : KINDS * 3 * BLOCKS]
+            )
+            nc.vector.tensor_scalar_mul(out=neg_bias[:], in0=bias, scalar1=-1.0)
+            nc.vector.tensor_add(out=rest[:], in0=bias, in1=shift)
+            nc.vector.tensor_scalar_mul(out=rest[:], in0=rest[:], scalar1=3.0)
+
+        w_grouped = {}
+        w_codes = {}
+        w_scales = {}
+
+        def regroup_weight(t):
+            if not 0 <= t < KINDS:
+                return
             grouped = stage.tile([P, D, PACK], BF16, align_bytes=64, name="w_grouped")
             nc.scalar.copy(
                 out=grouped[:].rearrange("p (c i) t -> p c t i", i=4),
                 in_=w_raw[t][:].rearrange("p t (c i) -> p c t i", i=4),
             )
-            codes = keep.tile([P, D], U32, align_bytes=64, name="w_codes%d" % t)
-            scales = keep.tile([P, D], U8, align_bytes=64, name="w_scales%d" % t)
-            nc.vector.quantize_mx(
-                out=codes[:].bitcast(FP8X4),
-                scales=scales[:],
-                in_=grouped[:].rearrange("p c t -> p (c t)"),
-            )
-            w_codes.append(codes)
-            w_scales.append(scales)
+            w_grouped[t] = grouped
 
+        def quantise_weight(t):
+            if not 0 <= t < KINDS:
+                return
+            w_codes[t] = keep.tile([P, D], U32, align_bytes=64, name="w_codes%d" % t)
+            w_scales[t] = keep.tile([P, D], U8, align_bytes=64, name="w_scales%d" % t)
+            nc.vector.quantize_mx(
+                out=w_codes[t][:].bitcast(FP8X4),
+                scales=w_scales[t][:],
+                in_=w_grouped[t][:].rearrange("p c t -> p (c t)"),
+            )
+
+        x_grouped = {}
         x_codes = {}
         x_scales = {}
+
+        def transpose_x(index):
+            if not 0 <= index < STEPS:
+                return
+            g, i, l = split(index)
+            words = x_sb[(g, l)][:].bitcast(F32)
+            xt = psum.tile([P, 2, P], F32, tag="xt", name="xt")
+            for u in range(2):
+                nc.tensor.transpose(xt[:, u, :], words[:, i, P * u : P * u + P], ident_f[:])
+            grouped = stage.tile([P, P, PACK], BF16, align_bytes=64, bufs=3, name="x_grouped")
+            nc.scalar.copy(out=grouped[:].bitcast(F32), in_=xt[:].rearrange("p u r -> p r u"))
+            x_grouped[index] = grouped
+
+        def quantise_x(index):
+            if not 0 <= index < STEPS:
+                return
+            g, i, l = split(index)
+            if i == 0:
+                x_codes[(g, l)] = stage.tile([P, TILES * P], U32, align_bytes=64, bufs=6, name="x_codes")
+                x_scales[(g, l)] = stage.tile([P, TILES * P], U8, align_bytes=64, bufs=6, name="x_scales")
+            nc.vector.quantize_mx(
+                out=x_codes[(g, l)][:, P * i : P * i + P].bitcast(FP8X4),
+                scales=x_scales[(g, l)][:, P * i : P * i + P],
+                in_=x_grouped[index][:].rearrange("p r t -> p (r t)"),
+            )
+
+        stats = {}
+        mean_var = {}
+        std = {}
+        rstd = {}
+        offset = {}
         normed = {}
+
+        def statistics(index):
+            if not 0 <= index < STEPS:
+                return
+            g, i, l = split(index)
+            if l == 0:
+                stats[(g, i)] = small.tile([P, LAYERS, 6], F32, name="stats")
+            nc.vector.bn_stats(out=stats[(g, i)][:, l, :], in_=x_sb[(g, l)][:, i, :])
+
+        def aggregate(index):
+            if not 0 <= index < STEPS:
+                return
+            g, i, l = split(index)
+            if l == 0:
+                mean_var[(g, i)] = small.tile([P, LAYERS, 2], F32, name="mean_var")
+            nc.vector.bn_aggr(out=mean_var[(g, i)][:, l, :], in_=stats[(g, i)][:, l, :])
+
+        def deviation(index):
+            if not 0 <= index < STEPS:
+                return
+            g, i, l = split(index)
+            if l == LAYERS - 1:
+                std[(g, i)] = small.tile([P, LAYERS], F32, name="std")
+                nc.scalar.activation(
+                    out=std[(g, i)][:], in_=mean_var[(g, i)][:, :, 1], func=ACT.Sqrt, bias=eps[:], scale=1.0
+                )
+
+        def reciprocal(index):
+            if not 0 <= index < STEPS:
+                return
+            g, i, l = split(index)
+            if l == LAYERS - 1:
+                rstd[(g, i)] = small.tile([P, LAYERS], F32, name="rstd")
+                nc.vector.reciprocal(out=rstd[(g, i)][:], in_=std[(g, i)][:])
+                offset[(g, i)] = small.tile([P, LAYERS], F32, name="offset")
+                nc.vector.scalar_tensor_tensor(
+                    out=offset[(g, i)][:], in0=mean_var[(g, i)][:, :, 0], scalar=-1.0, in1=rstd[(g, i)][:],
+                    op0=ALU.mult, op1=ALU.mult,
+                )
+
+        def scale(index):
+            if not 0 <= index < STEPS:
+                return
+            g, i, l = split(index)
+            y = stage.tile([P, D], F32, bufs=2 * PER_GROUP, name="normed")
+            nc.gpsimd.tensor_scalar(
+                out=y[:], in0=x_sb[(g, l)][:, i, :],
+                scalar1=rstd[(g, i)][:, l : l + 1], scalar2=offset[(g, i)][:, l : l + 1],
+                op0=ALU.mult, op1=ALU.add,
+            )
+            normed[(g, i, l)] = y
+
+        nt = {}
         acc = {}
 
-        def quantise_group(g):
-            for l in range(LAYERS):
-                words = x_sb[(g, l)][:].bitcast(F32)
-                grouped = stage.tile([P, TILES * P, PACK], BF16, align_bytes=64, bufs=3, name="x_grouped")
-                grouped_words = grouped[:].bitcast(F32)
-                for pair in range(TILES // 2):
-                    xt = psum.tile([P, 2, 2, P], F32, tag="xt", bufs=1, name="xt")
-                    for i in range(2):
-                        for u in range(2):
-                            nc.tensor.transpose(
-                                xt[:, i, u, :], words[:, 2 * pair + i, P * u : P * u + P], ident_f[:]
-                            )
-                    nc.scalar.copy(
-                        out=grouped_words[:, 2 * P * pair : 2 * P * pair + 2 * P, :].rearrange(
-                            "p (i r) u -> p i r u", i=2
-                        ),
-                        in_=xt[:].rearrange("p i u r -> p i r u"),
-                    )
-                codes = stage.tile([P, TILES * P], U32, align_bytes=64, bufs=6, name="x_codes")
-                scales = stage.tile([P, TILES * P], U8, align_bytes=64, bufs=6, name="x_scales")
-                nc.vector.quantize_mx(
-                    out=codes[:].bitcast(FP8X4),
-                    scales=scales[:],
-                    in_=grouped[:].rearrange("p n t -> p (n t)"),
+        def transpose_normed(index):
+            if not 0 <= index < STEPS:
+                return
+            g, j, third = split(index)
+            if third == 0:
+                nt[(g, j)] = psum.tile([P, TILES * P], F32, tag="nt", bufs=2, name="nt")
+            for n in range(TILES * third, TILES * third + TILES):
+                i, l = divmod(n, LAYERS)
+                nc.tensor.matmul(
+                    out=nt[(g, j)][:, P * i : P * i + P],
+                    lhsT=normed[(g, i, l)][:, P * j : P * j + P],
+                    rhs=ident_f[:],
+                    is_transpose=True,
+                    start=(l == 0),
+                    stop=(l == LAYERS - 1),
                 )
-                x_codes[(g, l)] = codes
-                x_scales[(g, l)] = scales
 
-        def normalise_group(g):
-            for l in range(LAYERS):
-                stats = small.tile([P, TILES, 6], F32, name="stats")
-                mean_var = small.tile([P, TILES, 2], F32, name="mean_var")
-                for i in range(TILES):
-                    nc.vector.bn_stats(out=stats[:, i, :], in_=x_sb[(g, l)][:, i, :])
-                for i in range(TILES):
-                    nc.vector.bn_aggr(out=mean_var[:, i, :], in_=stats[:, i, :])
-                std = small.tile([P, TILES], F32, name="std")
-                nc.scalar.activation(out=std[:], in_=mean_var[:, :, 1], func=ACT.Sqrt, bias=eps[:], scale=1.0)
-                rstd = small.tile([P, TILES], F32, name="rstd")
-                nc.vector.reciprocal(out=rstd[:], in_=std[:])
-                offset = small.tile([P, TILES], F32, name="offset")
-                nc.vector.scalar_tensor_tensor(
-                    out=offset[:], in0=mean_var[:, :, 0], scalar=-1.0, in1=rstd[:], op0=ALU.mult, op1=ALU.mult
-                )
-                for i in range(TILES):
-                    y = stage.tile([P, D], F32, bufs=2 * LAYERS * TILES, name="normed")
-                    nc.gpsimd.tensor_scalar(
-                        out=y[:], in0=x_sb[(g, l)][:, i, :],
-                        scalar1=rstd[:, i : i + 1], scalar2=offset[:, i : i + 1],
-                        op0=ALU.mult, op1=ALU.add,
-                    )
-                    normed[(g, l, i)] = y
+        def seed(index):
+            if not 0 <= index < STEPS:
+                return
+            g, j, t = split(index)
+            a = stage.tile([P, TILES * P], F32, bufs=10, name="acc")
+            nc.scalar.activation(
+                out=a[:], in_=nt[(g, j)][:], func=ACT.Identity,
+                scale=gain[:, t, j : j + 1], bias=rest[:, t, j : j + 1],
+            )
+            acc[(g, t, j)] = a
 
-        def seed_group(g):
-            for j in range(BLOCKS):
-                nt = psum.tile([P, TILES * P], F32, tag="nt", bufs=2, name="nt")
-                for i in range(TILES):
-                    for l in range(LAYERS):
-                        nc.tensor.matmul(
-                            out=nt[:, P * i : P * i + P],
-                            lhsT=normed[(g, l, i)][:, P * j : P * j + P],
-                            rhs=ident_f[:],
-                            is_transpose=True,
-                            start=(l == 0),
-                            stop=(l == LAYERS - 1),
-                        )
-                for t in range(KINDS):
-                    a = stage.tile([P, TILES * P], F32, bufs=2 * KINDS * BLOCKS, name="acc")
-                    nc.scalar.activation(
-                        out=a[:], in_=nt[:], func=ACT.Identity,
-                        scale=gain[:, t, j : j + 1], bias=rest[:, t, j : j + 1],
-                    )
-                    acc[(g, t, j)] = a
-
-        def products_group(g):
-            b, h = groups[g]
+        def products(index):
+            if not 0 <= index < STEPS:
+                return
+            g, j, l = split(index)
+            cols = slice(P * j, P * j + P)
             for t in range(KINDS):
-                for l in range(LAYERS):
-                    for j in range(BLOCKS):
-                        cols = slice(P * j, P * j + P)
-                        prod = psum.tile([P, TILES * P], F32, tag="prod", bufs=3, name="prod")
-                        nc.tensor.matmul_mx(
-                            out=prod[:],
-                            lhsT=w_codes[t][:, cols].bitcast(FP8X4),
-                            lhsT_scale=w_scales[t][:, cols],
-                            rhs=x_codes[(g, l)][:].bitcast(FP8X4),
-                            rhs_scale=x_scales[(g, l)][:],
-                            start=True,
-                            stop=True,
-                        )
-                        nc.vector.scalar_tensor_tensor(
-                            out=acc[(g, t, j)][:], in0=prod[:], scalar=neg_bias[:, t, j : j + 1],
-                            in1=acc[(g, t, j)][:], op0=ALU.max, op1=ALU.add,
-                        )
-                for i in range(TILES):
-                    back = psum.tile([P, D], F32, tag="back", bufs=2, name="back")
-                    for j in range(BLOCKS):
-                        nc.tensor.transpose(
-                            back[:, P * j : P * j + P], acc[(g, t, j)][:, P * i : P * i + P], ident_f[:]
-                        )
-                    result = stage.tile([P, D], F32, bufs=6, name="result")
-                    nc.scalar.copy(out=result[:], in_=back[:])
-                    nc.sync.dma_start(out=rows_of_group(outs[t][b], h)[:, i], in_=result[:])
+                prod = psum.tile([P, TILES * P], F32, tag="prod", bufs=3, name="prod")
+                nc.tensor.matmul_mx(
+                    out=prod[:],
+                    lhsT=w_codes[t][:, cols].bitcast(FP8X4),
+                    lhsT_scale=w_scales[t][:, cols],
+                    rhs=x_codes[(g, l)][:].bitcast(FP8X4),
+                    rhs_scale=x_scales[(g, l)][:],
+                    start=True,
+                    stop=True,
+                )
+                nc.vector.scalar_tensor_tensor(
+                    out=acc[(g, t, j)][:], in0=prod[:], scalar=neg_bias[:, t, j : j + 1],
+                    in1=acc[(g, t, j)][:], op0=ALU.max, op1=ALU.add,
+                )
 
-        normalise_group(0)
-        normalise_group(1)
-        quantise_group(0)
-        seed_group(0)
-        for g in range(len(groups)):
-            if g + 2 < len(groups):
-                normalise_group(g + 2)
-            if g + 1 < len(groups):
-                quantise_group(g + 1)
-                seed_group(g + 1)
-            products_group(g)
+        def back(index):
+            if not 0 <= index < STEPS:
+                return
+            g, j, t = split(index)
+            turned = psum.tile([P, TILES, P], F32, tag="back", bufs=2, name="turned")
+            for i in range(TILES):
+                nc.tensor.transpose(turned[:, i, :], acc[(g, t, j)][:, P * i : P * i + P], ident_f[:])
+            result = stage.tile([P, TILES, P], F32, bufs=4, name="result")
+            nc.scalar.copy(out=result[:], in_=turned[:])
+            nc.sync.dma_start(out=rows_of_group(outs[t], g)[:, :, P * j : P * j + P], in_=result[:])
+
+        for step in range(-LEAD_STATS, STEPS + LAG_BACK):
+            products(step)
+            deviation(step + LEAD_STD)
+            seed(step + LEAD_SEED)
+            back(step - LAG_BACK)
+            transpose_normed(step + LEAD_NT)
+            transpose_x(step + LEAD_XT)
+            regroup_weight(step + LEAD_WEIGHTS)
+            constants(step + LEAD_CONSTANTS)
+            statistics(step + LEAD_STATS)
+            quantise_x(step + LEAD_QUANTISE)
+            quantise_weight(step + LEAD_WEIGHTS - 1)
+            aggregate(step + LEAD_STATS)
+            reciprocal(step + LEAD_RSTD)
+            scale(step + LEAD_SCALE)

@@ -30,7 +30,7 @@ LEAD_RSTD = 22
 LEAD_STD = 23
 LEAD_STATS = 24
 LEAD_QUANTISE = 11
-LEAD_XT = 12
+LEAD_XT = 24
 LEAD_WEIGHTS = 14
 LEAD_CONSTANTS = 8
 LAG_BACK = 3
@@ -111,7 +111,7 @@ def tile_dcadecoderblock_pa_t_kernel(
         def constants(index):
             if index != 0:
                 return
-            vec_ps = psum.tile([P, P], BF16, tag="xt", name="vec_ps")
+            vec_ps = psum.tile([P, P], BF16, tag="xt", bufs=2, name="vec_ps")
             nc.tensor.transpose(vec_ps[:], vec_rows[:], ident_b[:])
             nc.vector.tensor_copy(
                 out=vec_cols[:].rearrange("p t v j -> p (t v j)"), in_=vec_ps[:, 0 : KINDS * 3 * BLOCKS]
@@ -154,24 +154,27 @@ def tile_dcadecoderblock_pa_t_kernel(
                 return
             g, i, l = split(index)
             words = x_sb[(g, l)][:].bitcast(F32)
-            xt = psum.tile([P, 2, P], F32, tag="xt", name="xt")
+            xt = psum.tile([P, 2, P], F32, tag="xt", bufs=2, name="xt")
             for u in range(2):
                 nc.tensor.transpose(xt[:, u, :], words[:, i, P * u : P * u + P], ident_f[:])
-            grouped = stage.tile([P, P, PACK], BF16, align_bytes=64, bufs=3, name="x_grouped")
-            nc.scalar.copy(out=grouped[:].bitcast(F32), in_=xt[:].rearrange("p u r -> p r u"))
-            x_grouped[index] = grouped
+            if i == 0:
+                x_grouped[(g, l)] = stage.tile([P, TILES * P, PACK], BF16, align_bytes=64, bufs=7, name="x_grouped")
+            nc.scalar.copy(
+                out=x_grouped[(g, l)][:, P * i : P * i + P, :].bitcast(F32), in_=xt[:].rearrange("p u r -> p r u")
+            )
 
         def quantise_x(index):
             if not 0 <= index < STEPS:
                 return
             g, i, l = split(index)
-            if i == 0:
-                x_codes[(g, l)] = stage.tile([P, TILES * P], U32, align_bytes=64, bufs=6, name="x_codes")
-                x_scales[(g, l)] = stage.tile([P, TILES * P], U8, align_bytes=64, bufs=6, name="x_scales")
+            if i < TILES - 1:
+                return
+            x_codes[(g, l)] = stage.tile([P, TILES * P], U32, align_bytes=64, bufs=6, name="x_codes")
+            x_scales[(g, l)] = stage.tile([P, TILES * P], U8, align_bytes=64, bufs=6, name="x_scales")
             nc.vector.quantize_mx(
-                out=x_codes[(g, l)][:, P * i : P * i + P].bitcast(FP8X4),
-                scales=x_scales[(g, l)][:, P * i : P * i + P],
-                in_=x_grouped[index][:].rearrange("p r t -> p (r t)"),
+                out=x_codes[(g, l)][:].bitcast(FP8X4),
+                scales=x_scales[(g, l)][:],
+                in_=x_grouped[(g, l)][:].rearrange("p r t -> p (r t)"),
             )
 
         stats = {}
@@ -288,14 +291,14 @@ def tile_dcadecoderblock_pa_t_kernel(
             if not 0 <= index < STEPS:
                 return
             g, j, t = split(index)
-            turned = psum.tile([P, TILES, P], F32, tag="back", bufs=2, name="turned")
+            turned = psum.tile([P, TILES, P], F32, tag="back", name="turned")
             for i in range(TILES):
                 nc.tensor.transpose(turned[:, i, :], acc[(g, t, j)][:, P * i : P * i + P], ident_f[:])
             result = stage.tile([P, TILES, P], F32, bufs=4, name="result")
             nc.scalar.copy(out=result[:], in_=turned[:])
             nc.sync.dma_start(out=rows_of_group(outs[t], g)[:, :, P * j : P * j + P], in_=result[:])
 
-        for step in range(-LEAD_STATS, STEPS + LAG_BACK):
+        for step in range(-LEAD_XT, STEPS + LAG_BACK):
             products(step)
             deviation(step + LEAD_STD)
             seed(step + LEAD_SEED)

from contextlib import ExitStack

import concourse.mybir as mybir
from concourse.masks import make_identity

F32 = mybir.dt.float32
BF16 = mybir.dt.bfloat16
U32 = mybir.dt.uint32
U8 = mybir.dt.uint8
FP8X4 = mybir.dt.float8_e4m3fn_x4
ALU = mybir.AluOpType
ACT = mybir.ActivationFunctionType

BATCH, LAYERS, SEQ, D = 2, 3, 1024, 512
EPS = 1e-5
P = 128
PACK = 4
TILES = 4
HALVES = SEQ // (P * TILES)
GROUPS = BATCH * HALVES
BLOCKS = D // P
KINDS = 3
PER_GROUP = BLOCKS * LAYERS
STEPS = GROUPS * PER_GROUP

LEAD_SEED = 3
LEAD_NT = 6
LEAD_SCALE = 19
LEAD_RSTD = 22
LEAD_STD = 23
LEAD_STATS = 24
LEAD_QUANTISE = 11
LEAD_XT = 24
LEAD_WEIGHTS = 14
LEAD_CONSTANTS = 8
LAG_BACK = 3

FLOPS = 2 * BATCH * LAYERS * SEQ * D * KINDS * D


def tile_dcadecoderblock_pa_t_kernel(
    tc,
    layer_outputs,
    grn_q_W, grn_q_b, grn_q_g, grn_q_be,
    grn_k_W, grn_k_b, grn_k_g, grn_k_be,
    grn_v_W, grn_v_b, grn_v_g, grn_v_be,
    out_0, out_1, out_2,
):
    nc = tc.nc
    weights = [grn_q_W, grn_k_W, grn_v_W]
    vectors = [grn_q_b, grn_q_g, grn_q_be, grn_k_b, grn_k_g, grn_k_be, grn_v_b, grn_v_g, grn_v_be]
    outs = [out_0, out_1, out_2]

    with ExitStack() as stack:
        stack.enter_context(tc.manual_schedule())
        keep = stack.enter_context(tc.tile_pool(name="keep", bufs=1))
        stage = stack.enter_context(tc.tile_pool(name="stage", bufs=2))
        small = stack.enter_context(tc.tile_pool(name="small", bufs=4))
        psum = stack.enter_context(tc.psum_pool(name="psum", bufs=1))

        def rows_of_group(dram, g):
            return dram[g // HALVES].rearrange("(p h i) f -> p h i f", h=HALVES, i=TILES)[:, g % HALVES]

        x_sb = {}

        def load_group(g):
            for l in range(LAYERS):
                x = keep.tile([P, TILES, D], BF16, name="x%d_%d" % (g, l))
                nc.sync.dma_start(out=x[:], in_=rows_of_group(layer_outputs[:, l], g))
                x_sb[(g, l)] = x

        load_group(0)
        w_raw = []
        for t in range(KINDS):
            raw = keep.tile([P, PACK, D], BF16, name="w_raw%d" % t)
            for u in range(2):
                nc.sync.dma_start(
                    out=raw[:, 2 * u : 2 * u + 2, :],
                    in_=weights[t][256 * u : 256 * u + 256, :].rearrange("(p e) c -> p e c", e=2),
                )
            w_raw.append(raw)
        vec_rows = keep.tile([P, P], BF16, name="vec_rows")
        nc.vector.memset(vec_rows[:], 0.0)
        for n, vec in enumerate(vectors):
            nc.sync.dma_start(
                out=vec_rows[BLOCKS * n : BLOCKS * n + BLOCKS, :],
                in_=vec.rearrange("(j p) -> j p", p=P),
            )
        for g in range(1, GROUPS):
            load_group(g)

        ident_f = keep.tile([P, P], F32, name="ident_f")
        make_identity(nc, ident_f[:])
        ident_b = keep.tile([P, P], BF16, name="ident_b")
        make_identity(nc, ident_b[:])
        eps = keep.tile([P, 1], F32, name="eps")
        nc.vector.memset(eps[:], EPS)

        vec_cols = keep.tile([P, KINDS, 3, BLOCKS], F32, name="vec_cols")
        bias = vec_cols[:, :, 0, :]
        gain = vec_cols[:, :, 1, :]
        shift = vec_cols[:, :, 2, :]
        neg_bias = keep.tile([P, KINDS, BLOCKS], F32, name="neg_bias")
        rest = keep.tile([P, KINDS, BLOCKS], F32, name="rest")

        def split(index):
            g, within = divmod(index, PER_GROUP)
            a, c = divmod(within, LAYERS)
            return g, a, c

        def constants(index):
            if index != 0:
                return
            vec_ps = psum.tile([P, P], BF16, tag="xt", bufs=2, name="vec_ps")
            nc.tensor.transpose(vec_ps[:], vec_rows[:], ident_b[:])
            nc.vector.tensor_copy(
                out=vec_cols[:].rearrange("p t v j -> p (t v j)"), in_=vec_ps[:, 0 : KINDS * 3 * BLOCKS]
            )
            nc.vector.tensor_scalar_mul(out=neg_bias[:], in0=bias, scalar1=-1.0)
            nc.vector.tensor_add(out=rest[:], in0=bias, in1=shift)
            nc.vector.tensor_scalar_mul(out=rest[:], in0=rest[:], scalar1=3.0)

        w_grouped = {}
        w_codes = {}
        w_scales = {}

        def regroup_weight(t):
            if not 0 <= t < KINDS:
                return
            grouped = stage.tile([P, D, PACK], BF16, align_bytes=64, name="w_grouped")
            nc.scalar.copy(
                out=grouped[:].rearrange("p (c i) t -> p c t i", i=4),
                in_=w_raw[t][:].rearrange("p t (c i) -> p c t i", i=4),
            )
            w_grouped[t] = grouped

        def quantise_weight(t):
            if not 0 <= t < KINDS:
                return
            w_codes[t] = keep.tile([P, D], U32, align_bytes=64, name="w_codes%d" % t)
            w_scales[t] = keep.tile([P, D], U8, align_bytes=64, name="w_scales%d" % t)
            nc.vector.quantize_mx(
                out=w_codes[t][:].bitcast(FP8X4),
                scales=w_scales[t][:],
                in_=w_grouped[t][:].rearrange("p c t -> p (c t)"),
            )

        x_grouped = {}
        x_codes = {}
        x_scales = {}

        def transpose_x(index):
            if not 0 <= index < STEPS:
                return
            g, i, l = split(index)
            words = x_sb[(g, l)][:].bitcast(F32)
            xt = psum.tile([P, 2, P], F32, tag="xt", bufs=2, name="xt")
            for u in range(2):
                nc.tensor.transpose(xt[:, u, :], words[:, i, P * u : P * u + P], ident_f[:])
            if i == 0:
                x_grouped[(g, l)] = stage.tile([P, TILES * P, PACK], BF16, align_bytes=64, bufs=7, name="x_grouped")
            nc.scalar.copy(
                out=x_grouped[(g, l)][:, P * i : P * i + P, :].bitcast(F32), in_=xt[:].rearrange("p u r -> p r u")
            )

        def quantise_x(index):
            if not 0 <= index < STEPS:
                return
            g, i, l = split(index)
            if i < TILES - 1:
                return
            x_codes[(g, l)] = stage.tile([P, TILES * P], U32, align_bytes=64, bufs=6, name="x_codes")
            x_scales[(g, l)] = stage.tile([P, TILES * P], U8, align_bytes=64, bufs=6, name="x_scales")
            nc.vector.quantize_mx(
                out=x_codes[(g, l)][:].bitcast(FP8X4),
                scales=x_scales[(g, l)][:],
                in_=x_grouped[(g, l)][:].rearrange("p r t -> p (r t)"),
            )

        stats = {}
        mean_var = {}
        std = {}
        rstd = {}
        offset = {}
        normed = {}

        def statistics(index):
            if not 0 <= index < STEPS:
                return
            g, i, l = split(index)
            if l == 0:
                stats[(g, i)] = small.tile([P, LAYERS, 6], F32, name="stats")
            nc.vector.bn_stats(out=stats[(g, i)][:, l, :], in_=x_sb[(g, l)][:, i, :])

        def aggregate(index):
            if not 0 <= index < STEPS:
                return
            g, i, l = split(index)
            if l == 0:
                mean_var[(g, i)] = small.tile([P, LAYERS, 2], F32, name="mean_var")
            nc.vector.bn_aggr(out=mean_var[(g, i)][:, l, :], in_=stats[(g, i)][:, l, :])

        def deviation(index):
            if not 0 <= index < STEPS:
                return
            g, i, l = split(index)
            if l == LAYERS - 1:
                std[(g, i)] = small.tile([P, LAYERS], F32, name="std")
                nc.scalar.activation(
                    out=std[(g, i)][:], in_=mean_var[(g, i)][:, :, 1], func=ACT.Sqrt, bias=eps[:], scale=1.0
                )

        def reciprocal(index):
            if not 0 <= index < STEPS:
                return
            g, i, l = split(index)
            if l == LAYERS - 1:
                rstd[(g, i)] = small.tile([P, LAYERS], F32, name="rstd")
                nc.vector.reciprocal(out=rstd[(g, i)][:], in_=std[(g, i)][:])
                offset[(g, i)] = small.tile([P, LAYERS], F32, name="offset")
                nc.vector.scalar_tensor_tensor(
                    out=offset[(g, i)][:], in0=mean_var[(g, i)][:, :, 0], scalar=-1.0, in1=rstd[(g, i)][:],
                    op0=ALU.mult, op1=ALU.mult,
                )

        def scale(index):
            if not 0 <= index < STEPS:
                return
            g, i, l = split(index)
            y = stage.tile([P, D], F32, bufs=2 * PER_GROUP, name="normed")
            nc.gpsimd.tensor_scalar(
                out=y[:], in0=x_sb[(g, l)][:, i, :],
                scalar1=rstd[(g, i)][:, l : l + 1], scalar2=offset[(g, i)][:, l : l + 1],
                op0=ALU.mult, op1=ALU.add,
            )
            normed[(g, i, l)] = y

        nt = {}
        acc = {}

        def transpose_normed(index):
            if not 0 <= index < STEPS:
                return
            g, j, third = split(index)
            if third == 0:
                nt[(g, j)] = psum.tile([P, TILES * P], F32, tag="nt", bufs=2, name="nt")
            for n in range(TILES * third, TILES * third + TILES):
                i, l = divmod(n, LAYERS)
                nc.tensor.matmul(
                    out=nt[(g, j)][:, P * i : P * i + P],
                    lhsT=normed[(g, i, l)][:, P * j : P * j + P],
                    rhs=ident_f[:],
                    is_transpose=True,
                    start=(l == 0),
                    stop=(l == LAYERS - 1),
                )

        def seed(index):
            if not 0 <= index < STEPS:
                return
            g, j, t = split(index)
            a = stage.tile([P, TILES * P], F32, bufs=10, name="acc")
            nc.scalar.activation(
                out=a[:], in_=nt[(g, j)][:], func=ACT.Identity,
                scale=gain[:, t, j : j + 1], bias=rest[:, t, j : j + 1],
            )
            acc[(g, t, j)] = a

        def products(index):
            if not 0 <= index < STEPS:
                return
            g, j, l = split(index)
            cols = slice(P * j, P * j + P)
            for t in range(KINDS):
                prod = psum.tile([P, TILES * P], F32, tag="prod", bufs=3, name="prod")
                nc.tensor.matmul_mx(
                    out=prod[:],
                    lhsT=w_codes[t][:, cols].bitcast(FP8X4),
                    lhsT_scale=w_scales[t][:, cols],
                    rhs=x_codes[(g, l)][:].bitcast(FP8X4),
                    rhs_scale=x_scales[(g, l)][:],
                    start=True,
                    stop=True,
                )
                nc.vector.scalar_tensor_tensor(
                    out=acc[(g, t, j)][:], in0=prod[:], scalar=neg_bias[:, t, j : j + 1],
                    in1=acc[(g, t, j)][:], op0=ALU.max, op1=ALU.add,
                )

        def back(index):
            if not 0 <= index < STEPS:
                return
            g, j, t = split(index)
            turned = psum.tile([P, TILES, P], F32, tag="back", name="turned")
            for i in range(TILES):
                nc.tensor.transpose(turned[:, i, :], acc[(g, t, j)][:, P * i : P * i + P], ident_f[:])
            result = stage.tile([P, TILES, P], F32, bufs=4, name="result")
            nc.scalar.copy(out=result[:], in_=turned[:])
            nc.sync.dma_start(out=rows_of_group(outs[t], g)[:, :, P * j : P * j + P], in_=result[:])

        for step in range(-LEAD_XT, STEPS + LAG_BACK):
            products(step)
            deviation(step + LEAD_STD)
            seed(step + LEAD_SEED)
            back(step - LAG_BACK)
            transpose_normed(step + LEAD_NT)
            transpose_x(step + LEAD_XT)
            regroup_weight(step + LEAD_WEIGHTS)
            constants(step + LEAD_CONSTANTS)
            statistics(step + LEAD_STATS)
            quantise_x(step + LEAD_QUANTISE)
            quantise_weight(step + LEAD_WEIGHTS - 1)
            aggregate(step + LEAD_STATS)
            reciprocal(step + LEAD_RSTD)
            scale(step + LEAD_SCALE)
